import numpy as np
import ml_dtypes


def mxq(x, axis, fmt="e4m3"):
    dtype, down = {"e4m3": (ml_dtypes.float8_e4m3fn, 7), "e5m2": (ml_dtypes.float8_e5m2, 14)}[fmt]
    v = np.moveaxis(np.asarray(x, np.float32).astype(ml_dtypes.bfloat16).astype(np.float64), axis, -1)
    blocks = v.reshape(v.shape[:-1] + (-1, 32))
    amax = np.abs(blocks).max(-1, keepdims=True)
    byte = np.maximum(np.where(amax > 0, np.frexp(amax)[1] - 1 + 127, 0) - down, 1)
    scale = np.exp2(byte - 127.0)
    codes = (blocks / scale).astype(np.float32).astype(dtype).astype(np.float64)
    return np.moveaxis((codes * scale).reshape(v.shape), -1, axis)


WIDE = False


def mx_kscale(k):
    if not WIDE:
        return np.ones(k)
    levels = np.array([10, -10, 5, -5, 0])
    a = np.random.permutation(np.resize(levels, k // 512 * 4)).reshape(k // 512, 4)
    idx = np.arange(k)
    return np.exp2(a[idx // 512, idx % 128 // 32])


BF16 = ml_dtypes.bfloat16


def bf(x):
    return np.asarray(x, np.float32).astype(BF16)


def f64(x):
    return np.asarray(x).astype(np.float64)


E2M1 = np.array([0.0, 0.5, 1.0, 1.5, 2.0, 3.0, 4.0, 6.0, -0.0, -0.5, -1.0, -1.5, -2.0, -3.0, -4.0, -6.0])


def pack_weight(w, fmt):
    k, n = w.shape
    w = f64(bf(w)).reshape(k // 32, 32, n)
    amax = np.abs(w).max(1)
    if fmt == "e4m3":
        byte = np.frexp(amax)[1] - 1 + 127 - 7
    else:
        mant, ex = np.frexp(amax / 6.0)
        byte = np.where(mant > 0.5, ex, ex - 1) + 127
    byte = np.clip(np.where(amax > 0, byte, 1), 1, 254)
    scaled = (w * np.exp2(127.0 - byte)[:, None, :]).reshape(k, n).astype(np.float32)
    by_word = np.ascontiguousarray(scaled.reshape(k // 512, 128, 4, n).transpose(0, 1, 3, 2))
    if fmt == "e4m3":
        words = by_word.astype(ml_dtypes.float8_e4m3fn).view(np.uint8)
    else:
        c = by_word.astype(ml_dtypes.float4_e2m1fn).view(np.uint8) & 0xF
        words = c[..., 0::2] | (c[..., 1::2] << 4)
    return np.ascontiguousarray(words), np.ascontiguousarray(byte.astype(np.uint8).reshape(k // 512, 16, n))


def unpack_weight(words, scales, fmt):
    g, p, n, _ = words.shape
    if fmt == "e4m3":
        vals = np.ascontiguousarray(words).view(ml_dtypes.float8_e4m3fn).astype(np.float64)
    else:
        nib = np.empty((g, p, n, 4), np.uint8)
        nib[..., 0::2] = words & 0xF
        nib[..., 1::2] = words >> 4
        vals = E2M1[nib]
    vals = vals * np.repeat(np.exp2(scales.astype(np.float64) - 127.0), 8, axis=1)[..., None]
    return vals.transpose(0, 1, 3, 2).reshape(g * 512, n)


G, B, D, F, O = 4, 256, 512, 2048, 512


def silu(v):
    return v / (1.0 + np.exp(-v))


def setup_inputs():
    s, t = mx_kscale(D), mx_kscale(F)
    x = bf(np.random.standard_normal((B * G, D)) * s)
    gate_stack = np.random.standard_normal((G, D, F)) / np.sqrt(D) / s[:, None]
    up_stack = np.random.standard_normal((G, D, F)) / np.sqrt(D) / s[:, None] * t
    down_stack = np.random.standard_normal((G, F, O)) * 1.5 / np.sqrt(F) / t[:, None]
    gate_words, gate_scales = pack_weight(gate_stack.reshape(-1, F), "e4m3")
    up_words, up_scales = pack_weight(up_stack.reshape(-1, F), "e4m3")
    down_words, down_scales = pack_weight(down_stack.reshape(-1, O), "e4m3")
    return {"x": x,
            "gate_weight_words": gate_words, "gate_weight_scales": gate_scales,
            "up_weight_words": up_words, "up_weight_scales": up_scales,
            "down_weight_words": down_words, "down_weight_scales": down_scales}


def reference(x, gate_weight_words, gate_weight_scales, up_weight_words, up_weight_scales, down_weight_words, down_weight_scales):
    num_groups = G
    input_dim = D
    batch = x.shape[0] // num_groups
    xb = f64(x).reshape(batch, num_groups, input_dim)
    xq = mxq(xb, 2, "e4m3").transpose(1, 0, 2)
    gate = xq @ unpack_weight(gate_weight_words, gate_weight_scales, "e4m3").reshape(G, D, F)
    up = xq @ unpack_weight(up_weight_words, up_weight_scales, "e4m3").reshape(G, D, F)
    hidden = silu(gate) * up
    out = mxq(hidden, 2, "e4m3") @ unpack_weight(down_weight_words, down_weight_scales, "e4m3").reshape(G, F, O)
    return out.transpose(1, 0, 2).reshape(-1, O)

@@ -1,0 +1,230 @@
+from contextlib import ExitStack
+
+import concourse.mybir as mybir
+from concourse.masks import make_identity
+
+F32 = mybir.dt.float32
+BF16 = mybir.dt.bfloat16
+I32 = mybir.dt.int32
+U32 = mybir.dt.uint32
+U8 = mybir.dt.uint8
+FP8X4 = mybir.dt.float8_e4m3fn_x4
+SILU = mybir.ActivationFunctionType.Silu
+MULT = mybir.AluOpType.mult
+
+P = 128
+PACK = 4
+PAIRS = 2
+K_PASS = P * PACK
+QUADRANTS = 4
+
+GROUPS = 4
+ROWS = 256
+D_IN = 512
+D_HID = 2048
+D_OUT = 512
+ROW_TILES = ROWS // P
+CHUNKS = D_HID // K_PASS
+ROUNDS = GROUPS * CHUNKS
+
+FLOPS = 2 * GROUPS * ROWS * (2 * D_IN * D_HID + D_HID * D_OUT)
+
+
+def tile_groupedmlp_plana_e_kernel(
+    tc,
+    x,
+    gate_weight_words,
+    gate_weight_scales,
+    up_weight_words,
+    up_weight_scales,
+    down_weight_words,
+    down_weight_scales,
+    out,
+):
+    nc = tc.nc
+    with ExitStack() as ctx:
+        ctx.enter_context(tc.manual_schedule())
+        keep = ctx.enter_context(tc.tile_pool(name="keep", bufs=1))
+        work = ctx.enter_context(tc.tile_pool(name="work", bufs=2))
+
+        x_rows = keep.tile([P, ROW_TILES, GROUPS, D_IN], BF16)
+        x_words = keep.tile([P, GROUPS, ROWS], U32, align_bytes=64)
+        x_scales = keep.tile([P, GROUPS, ROWS], U8, align_bytes=64)
+        gate_words = keep.tile([P, GROUPS, D_HID], U32, align_bytes=64)
+        up_words = keep.tile([P, GROUPS, D_HID], U32, align_bytes=64)
+        down_words = keep.tile([P, ROUNDS, D_OUT], U32, align_bytes=64)
+        gate_scales = keep.tile([P, D_HID], U8, align_bytes=64)
+        up_scales = keep.tile([P, D_HID], U8, align_bytes=64)
+        down_scales = keep.tile([P, GROUPS, D_OUT], U8, align_bytes=64)
+        out_rows = keep.tile([P, ROW_TILES, GROUPS, D_OUT], F32)
+        identity = keep.tile([P, P], F32)
+        warm = keep.tile([P, 2], F32)
+
+        x_view = x.rearrange("(bt p g) d -> p bt g d", bt=ROW_TILES, p=P, g=GROUPS)
+        out_view = out.rearrange("(bt p g) o -> p bt g o", bt=ROW_TILES, p=P, g=GROUPS)
+
+        for planes in (gate_scales, up_scales, down_scales):
+            nc.vector.memset(planes[:].bitcast(I32), 0)
+        make_identity(nc, identity[:])
+        nc.vector.memset(warm[:], 0.0)
+        nc.scalar.activation(out=warm[:, 1:2], in_=warm[:, 0:1], func=SILU)
+
+        def load_planes(planes, scales):
+            for quadrant in range(QUADRANTS):
+                nc.sync.dma_start(
+                    out=planes[32 * quadrant : 32 * quadrant + 16, :].bitcast(I32),
+                    in_=scales[:, 4 * quadrant : 4 * quadrant + 4, :].bitcast(I32),
+                )
+
+        def load_gate_up(r):
+            g, c = divmod(r, CHUNKS)
+            for words, given in ((gate_words, gate_weight_words), (up_words, up_weight_words)):
+                given_bytes = given[g].rearrange("p n t -> p (n t)")
+                nc.sync.dma_start(
+                    out=words[:, g, K_PASS * c : K_PASS * (c + 1)].bitcast(I32),
+                    in_=given_bytes[:, PACK * K_PASS * c : PACK * K_PASS * (c + 1)].bitcast(I32),
+                )
+
+        def load_down(r):
+            g, c = divmod(r, CHUNKS)
+            if c == 0:
+                load_planes(down_scales[:, g, :], down_weight_scales[CHUNKS * g : CHUNKS * (g + 1)])
+            nc.sync.dma_start(
+                out=down_words[:, r, :].bitcast(I32),
+                in_=down_weight_words[r].rearrange("p n t -> p (n t)").bitcast(I32),
+            )
+
+        for bt in range(ROW_TILES):
+            nc.sync.dma_start(out=x_rows[:, bt], in_=x_view[:, bt])
+        load_planes(gate_scales, gate_weight_scales)
+        load_planes(up_scales, up_weight_scales)
+        for r in range(ROUNDS + 1):
+            if r < ROUNDS:
+                load_gate_up(r)
+            if r >= 1:
+                load_down(r - 1)
+
+        with tc.psum_pool(name="x_banks", bufs=GROUPS) as x_banks:
+            x_turned = [
+                x_banks.tile([P, ROW_TILES, PAIRS, P], F32, name="x_turned") for g in range(GROUPS)
+            ]
+            for bt in range(ROW_TILES):
+                for g in range(GROUPS):
+                    pair_words = x_rows[:, bt, g, :].bitcast(F32)
+                    for u in range(PAIRS):
+                        nc.tensor.transpose(
+                            x_turned[g][:, bt, u, :], pair_words[:, u : D_IN // 2 : PAIRS], identity[:]
+                        )
+            for g in range(GROUPS):
+                x_grouped = work.tile([P, ROW_TILES, P, PACK], BF16, align_bytes=64)
+                nc.scalar.copy(
+                    out=x_grouped[:].bitcast(F32),
+                    in_=x_turned[g][:].rearrange("p bt u b -> p bt b u"),
+                )
+                nc.vector.quantize_mx(
+                    out=x_words[:, g, :].bitcast(FP8X4),
+                    scales=x_scales[:, g, :],
+                    in_=x_grouped[:].rearrange("p bt b t -> p (bt b t)"),
+                )
+
+        gate_up_banks = ctx.enter_context(
+            tc.psum_pool(name="gate_up_banks", bufs=ROW_TILES, reuse_waits="tile")
+        )
+        turned_banks = ctx.enter_context(tc.psum_pool(name="turned_banks", bufs=2, reuse_waits="tile"))
+        down_banks = ctx.enter_context(
+            tc.psum_pool(name="down_banks", bufs=ROW_TILES, reuse_waits="tile")
+        )
+        gate_sums, up_sums, hidden, hidden_mx, down_sums = {}, {}, {}, {}, {}
+
+        def gate_up_passes(r):
+            g, c = divmod(r, CHUNKS)
+            cols = slice(K_PASS * c, K_PASS * (c + 1))
+            for sums, words, planes, name in (
+                (gate_sums, gate_words, gate_scales, "gate_bank"),
+                (up_sums, up_words, up_scales, "up_bank"),
+            ):
+                for bt in range(ROW_TILES):
+                    rows = slice(P * bt, P * (bt + 1))
+                    sums[bt] = gate_up_banks.tile([P, K_PASS], F32, name=name)
+                    nc.tensor.matmul_mx(
+                        out=sums[bt][:],
+                        lhsT=x_words[:, g, rows].bitcast(FP8X4),
+                        lhsT_scale=x_scales[:, g, rows],
+                        rhs=words[:, g, cols].bitcast(FP8X4),
+                        rhs_scale=planes[4 * g : P, cols],
+                        start=True,
+                        stop=True,
+                    )
+
+        def swiglu(r):
+            for bt in range(ROW_TILES):
+                silu_gate = work.tile([P, PAIRS, P, 2], F32)
+                nc.scalar.activation(
+                    out=silu_gate[:],
+                    in_=gate_sums[bt][:].rearrange("b (p u e) -> b u p e", u=PAIRS, e=2),
+                    func=SILU,
+                )
+                hidden[r, bt] = work.tile([P, PAIRS, P, 2], BF16, name="hidden", bufs=2 * ROW_TILES)
+                nc.vector.tensor_tensor(
+                    out=hidden[r, bt][:],
+                    in0=up_sums[bt][:].rearrange("b (p u e) -> b u p e", u=PAIRS, e=2),
+                    in1=silu_gate[:],
+                    op=MULT,
+                )
+
+        def turn_and_quantise_hidden(r):
+            turned = turned_banks.tile([P, ROW_TILES, PAIRS, P], F32)
+            for bt in range(ROW_TILES):
+                for u in range(PAIRS):
+                    nc.tensor.transpose(
+                        turned[:, bt, u, :],
+                        hidden[r, bt][:, u].rearrange("b p e -> b (p e)").bitcast(F32),
+                        identity[:],
+                    )
+            grouped = work.tile([P, ROW_TILES, P, PACK], BF16, align_bytes=64)
+            nc.scalar.copy(
+                out=grouped[:].bitcast(F32), in_=turned[:].rearrange("p bt u b -> p bt b u")
+            )
+            codes = work.tile([P, ROWS], U32, align_bytes=64)
+            scales = work.tile([P, ROWS], U8, align_bytes=64)
+            nc.vector.quantize_mx(
+                out=codes[:].bitcast(FP8X4),
+                scales=scales[:],
+                in_=grouped[:].rearrange("p bt b t -> p (bt b t)"),
+            )
+            hidden_mx[r] = (codes, scales)
+
+        def down_passes(r):
+            g, c = divmod(r, CHUNKS)
+            codes, scales = hidden_mx[r]
+            for bt in range(ROW_TILES):
+                rows = slice(P * bt, P * (bt + 1))
+                if c == 0:
+                    down_sums[bt] = down_banks.tile([P, D_OUT], F32, name="down_bank")
+                nc.tensor.matmul_mx(
+                    out=down_sums[bt][:],
+                    lhsT=codes[:, rows].bitcast(FP8X4),
+                    lhsT_scale=scales[:, rows],
+                    rhs=down_words[:, r, :].bitcast(FP8X4),
+                    rhs_scale=down_scales[4 * c : P, g, :],
+                    start=(c == 0),
+                    stop=(c == CHUNKS - 1),
+                )
+
+        def store_group(g):
+            nc.scalar.copy(out=out_rows[:, 0, g, :], in_=down_sums[0][:])
+            nc.vector.tensor_copy(out=out_rows[:, 1, g, :], in_=down_sums[1][:])
+            for bt in range(ROW_TILES):
+                nc.sync.dma_start(out=out_view[:, bt, g, :], in_=out_rows[:, bt, g, :])
+
+        for step in range(ROUNDS + 2):
+            if step < ROUNDS:
+                gate_up_passes(step)
+            if step >= 2:
+                down_passes(step - 2)
+            if step < ROUNDS:
+                swiglu(step)
+            if step >= 2 and (step - 2) % CHUNKS == CHUNKS - 1:
+                store_group((step - 2) // CHUNKS)
+            if 1 <= step <= ROUNDS:
+                turn_and_quantise_hidden(step - 1)

@@ -26,6 +26,7 @@ D_OUT = 512
 ROW_TILES = ROWS // P
 CHUNKS = D_HID // K_PASS
 ROUNDS = GROUPS * CHUNKS
+DOWN_LAG = 3
 
 FLOPS = 2 * GROUPS * ROWS * (2 * D_IN * D_HID + D_HID * D_OUT)
 
@@ -47,20 +48,20 @@ def tile_groupedmlp_plana_e_kernel(
         keep = ctx.enter_context(tc.tile_pool(name="keep", bufs=1))
         work = ctx.enter_context(tc.tile_pool(name="work", bufs=2))
 
-        x_rows = keep.tile([P, ROW_TILES, GROUPS, D_IN], BF16)
+        x_rows = keep.tile([P, GROUPS, ROW_TILES, D_IN], BF16)
         x_words = keep.tile([P, GROUPS, ROWS], U32, align_bytes=64)
         x_scales = keep.tile([P, GROUPS, ROWS], U8, align_bytes=64)
         gate_words = keep.tile([P, GROUPS, D_HID], U32, align_bytes=64)
         up_words = keep.tile([P, GROUPS, D_HID], U32, align_bytes=64)
         down_words = keep.tile([P, ROUNDS, D_OUT], U32, align_bytes=64)
-        gate_scales = keep.tile([P, D_HID], U8, align_bytes=64)
-        up_scales = keep.tile([P, D_HID], U8, align_bytes=64)
+        gate_scales = keep.tile([P, GROUPS, K_PASS], U8, align_bytes=64)
+        up_scales = keep.tile([P, GROUPS, K_PASS], U8, align_bytes=64)
         down_scales = keep.tile([P, GROUPS, D_OUT], U8, align_bytes=64)
         out_rows = keep.tile([P, ROW_TILES, GROUPS, D_OUT], F32)
         identity = keep.tile([P, P], F32)
         warm = keep.tile([P, 2], F32)
 
-        x_view = x.rearrange("(bt p g) d -> p bt g d", bt=ROW_TILES, p=P, g=GROUPS)
+        x_view = x.rearrange("(bt p g) d -> g p bt d", bt=ROW_TILES, p=P, g=GROUPS)
         out_view = out.rearrange("(bt p g) o -> p bt g o", bt=ROW_TILES, p=P, g=GROUPS)
 
         for planes in (gate_scales, up_scales, down_scales):
@@ -69,15 +70,23 @@ def tile_groupedmlp_plana_e_kernel(
         nc.vector.memset(warm[:], 0.0)
         nc.scalar.activation(out=warm[:, 1:2], in_=warm[:, 0:1], func=SILU)
 
-        def load_planes(planes, scales):
+        def load_planes(planes, four_planes):
             for quadrant in range(QUADRANTS):
                 nc.sync.dma_start(
                     out=planes[32 * quadrant : 32 * quadrant + 16, :].bitcast(I32),
-                    in_=scales[:, 4 * quadrant : 4 * quadrant + 4, :].bitcast(I32),
+                    in_=four_planes[:, 4 * quadrant : 4 * quadrant + 4, :].bitcast(I32),
                 )
 
         def load_gate_up(r):
             g, c = divmod(r, CHUNKS)
+            if c == 0:
+                for planes, given_scales in (
+                    (gate_scales, gate_weight_scales),
+                    (up_scales, up_weight_scales),
+                ):
+                    load_planes(
+                        planes[:, g, :], given_scales[g].rearrange("q (c n) -> c q n", c=CHUNKS)
+                    )
             for words, given in ((gate_words, gate_weight_words), (up_words, up_weight_words)):
                 given_bytes = given[g].rearrange("p n t -> p (n t)")
                 nc.sync.dma_start(
@@ -94,46 +103,18 @@ def tile_groupedmlp_plana_e_kernel(
                 in_=down_weight_words[r].rearrange("p n t -> p (n t)").bitcast(I32),
             )
 
-        for bt in range(ROW_TILES):
-            nc.sync.dma_start(out=x_rows[:, bt], in_=x_view[:, bt])
-        load_planes(gate_scales, gate_weight_scales)
-        load_planes(up_scales, up_weight_scales)
+        nc.sync.dma_start(out=x_rows[:, 0], in_=x_view[0])
         for r in range(ROUNDS + 1):
             if r < ROUNDS:
                 load_gate_up(r)
+            if 1 <= r < GROUPS:
+                nc.sync.dma_start(out=x_rows[:, r], in_=x_view[r])
             if r >= 1:
                 load_down(r - 1)
 
-        with tc.psum_pool(name="x_banks", bufs=GROUPS) as x_banks:
-            x_turned = [
-                x_banks.tile([P, ROW_TILES, PAIRS, P], F32, name="x_turned") for g in range(GROUPS)
-            ]
-            for bt in range(ROW_TILES):
-                for g in range(GROUPS):
-                    pair_words = x_rows[:, bt, g, :].bitcast(F32)
-                    for u in range(PAIRS):
-                        nc.tensor.transpose(
-                            x_turned[g][:, bt, u, :], pair_words[:, u : D_IN // 2 : PAIRS], identity[:]
-                        )
-            for g in range(GROUPS):
-                x_grouped = work.tile([P, ROW_TILES, P, PACK], BF16, align_bytes=64)
-                nc.scalar.copy(
-                    out=x_grouped[:].bitcast(F32),
-                    in_=x_turned[g][:].rearrange("p bt u b -> p bt b u"),
-                )
-                nc.vector.quantize_mx(
-                    out=x_words[:, g, :].bitcast(FP8X4),
-                    scales=x_scales[:, g, :],
-                    in_=x_grouped[:].rearrange("p bt b t -> p (bt b t)"),
-                )
-
-        gate_up_banks = ctx.enter_context(
-            tc.psum_pool(name="gate_up_banks", bufs=ROW_TILES, reuse_waits="tile")
-        )
-        turned_banks = ctx.enter_context(tc.psum_pool(name="turned_banks", bufs=2, reuse_waits="tile"))
-        down_banks = ctx.enter_context(
-            tc.psum_pool(name="down_banks", bufs=ROW_TILES, reuse_waits="tile")
-        )
+        gate_up_banks = ctx.enter_context(tc.psum_pool(name="gate_up_banks", bufs=ROW_TILES))
+        turned_banks = ctx.enter_context(tc.psum_pool(name="turned_banks", bufs=2))
+        down_banks = ctx.enter_context(tc.psum_pool(name="down_banks", bufs=ROW_TILES))
         gate_sums, up_sums, hidden, hidden_mx, down_sums = {}, {}, {}, {}, {}
 
         def gate_up_passes(r):
@@ -151,7 +132,7 @@ def tile_groupedmlp_plana_e_kernel(
                         lhsT=x_words[:, g, rows].bitcast(FP8X4),
                         lhsT_scale=x_scales[:, g, rows],
                         rhs=words[:, g, cols].bitcast(FP8X4),
-                        rhs_scale=planes[4 * g : P, cols],
+                        rhs_scale=planes[4 * c : P, g, :],
                         start=True,
                         stop=True,
                     )
@@ -172,25 +153,35 @@ def tile_groupedmlp_plana_e_kernel(
                     op=MULT,
                 )
 
-        def turn_and_quantise_hidden(r):
+        def turn_and_quantise(word_columns, codes, scales):
             turned = turned_banks.tile([P, ROW_TILES, PAIRS, P], F32)
             for bt in range(ROW_TILES):
                 for u in range(PAIRS):
-                    nc.tensor.transpose(
-                        turned[:, bt, u, :],
-                        hidden[r, bt][:, u].rearrange("b p e -> b (p e)").bitcast(F32),
-                        identity[:],
-                    )
+                    nc.tensor.transpose(turned[:, bt, u, :], word_columns(bt, u), identity[:])
             grouped = work.tile([P, ROW_TILES, P, PACK], BF16, align_bytes=64)
             nc.scalar.copy(
                 out=grouped[:].bitcast(F32), in_=turned[:].rearrange("p bt u b -> p bt b u")
             )
-            codes = work.tile([P, ROWS], U32, align_bytes=64)
-            scales = work.tile([P, ROWS], U8, align_bytes=64)
             nc.vector.quantize_mx(
-                out=codes[:].bitcast(FP8X4),
-                scales=scales[:],
+                out=codes.bitcast(FP8X4),
+                scales=scales,
                 in_=grouped[:].rearrange("p bt b t -> p (bt b t)"),
+            )
+
+        def turn_and_quantise_x(g):
+            turn_and_quantise(
+                lambda bt, u: x_rows[:, g, bt, :].bitcast(F32)[:, u : D_IN // 2 : PAIRS],
+                x_words[:, g, :],
+                x_scales[:, g, :],
+            )
+
+        def turn_and_quantise_hidden(r):
+            codes = work.tile([P, ROWS], U32, align_bytes=64, bufs=DOWN_LAG)
+            scales = work.tile([P, ROWS], U8, align_bytes=64, bufs=DOWN_LAG)
+            turn_and_quantise(
+                lambda bt, u: hidden[r, bt][:, u].rearrange("b p e -> b (p e)").bitcast(F32),
+                codes[:],
+                scales[:],
             )
             hidden_mx[r] = (codes, scales)
 
@@ -217,14 +208,17 @@ def tile_groupedmlp_plana_e_kernel(
             for bt in range(ROW_TILES):
                 nc.sync.dma_start(out=out_view[:, bt, g, :], in_=out_rows[:, bt, g, :])
 
-        for step in range(ROUNDS + 2):
+        turn_and_quantise_x(0)
+        for step in range(ROUNDS + DOWN_LAG):
             if step < ROUNDS:
                 gate_up_passes(step)
-            if step >= 2:
-                down_passes(step - 2)
+            if step >= DOWN_LAG:
+                down_passes(step - DOWN_LAG)
             if step < ROUNDS:
                 swiglu(step)
-            if step >= 2 and (step - 2) % CHUNKS == CHUNKS - 1:
-                store_group((step - 2) // CHUNKS)
+            if step >= DOWN_LAG and (step - DOWN_LAG) % CHUNKS == CHUNKS - 1:
+                store_group((step - DOWN_LAG) // CHUNKS)
             if 1 <= step <= ROUNDS:
                 turn_and_quantise_hidden(step - 1)
+            if 1 <= step < GROUPS:
+                turn_and_quantise_x(step)

@@ -51,9 +51,9 @@ def tile_groupedmlp_plana_e_kernel(
         x_rows = keep.tile([P, GROUPS, ROW_TILES, D_IN], BF16)
         x_words = keep.tile([P, GROUPS, ROWS], U32, align_bytes=64)
         x_scales = keep.tile([P, GROUPS, ROWS], U8, align_bytes=64)
-        gate_words = keep.tile([P, GROUPS, D_HID], U32, align_bytes=64)
-        up_words = keep.tile([P, GROUPS, D_HID], U32, align_bytes=64)
-        down_words = keep.tile([P, ROUNDS, D_OUT], U32, align_bytes=64)
+        gate_words = keep.tile([P, GROUPS, CHUNKS, K_PASS], U32, align_bytes=64)
+        up_words = keep.tile([P, GROUPS, CHUNKS, K_PASS], U32, align_bytes=64)
+        down_words = keep.tile([P, GROUPS, CHUNKS, D_OUT], U32, align_bytes=64)
         gate_scales = keep.tile([P, GROUPS, K_PASS], U8, align_bytes=64)
         up_scales = keep.tile([P, GROUPS, K_PASS], U8, align_bytes=64)
         down_scales = keep.tile([P, GROUPS, D_OUT], U8, align_bytes=64)
@@ -70,47 +70,56 @@ def tile_groupedmlp_plana_e_kernel(
         nc.vector.memset(warm[:], 0.0)
         nc.scalar.activation(out=warm[:, 1:2], in_=warm[:, 0:1], func=SILU)
 
-        def load_planes(planes, four_planes):
-            for quadrant in range(QUADRANTS):
-                nc.sync.dma_start(
-                    out=planes[32 * quadrant : 32 * quadrant + 16, :].bitcast(I32),
-                    in_=four_planes[:, 4 * quadrant : 4 * quadrant + 4, :].bitcast(I32),
-                )
+        gate = (
+            gate_words,
+            gate_scales,
+            gate_weight_words.rearrange("g p (c n) t -> g c p (n t)", c=CHUNKS),
+            gate_weight_scales.rearrange("g q (c n) -> g c q n", c=CHUNKS),
+        )
+        up = (
+            up_words,
+            up_scales,
+            up_weight_words.rearrange("g p (c n) t -> g c p (n t)", c=CHUNKS),
+            up_weight_scales.rearrange("g q (c n) -> g c q n", c=CHUNKS),
+        )
+        down = (
+            down_words,
+            down_scales,
+            down_weight_words.rearrange("(g c) p n t -> g c p (n t)", c=CHUNKS),
+            down_weight_scales.rearrange("(g c) q n -> g c q n", c=CHUNKS),
+        )
 
-        def load_gate_up(r):
-            g, c = divmod(r, CHUNKS)
-            if c == 0:
-                for planes, given_scales in (
-                    (gate_scales, gate_weight_scales),
-                    (up_scales, up_weight_scales),
-                ):
-                    load_planes(
-                        planes[:, g, :], given_scales[g].rearrange("q (c n) -> c q n", c=CHUNKS)
-                    )
-            for words, given in ((gate_words, gate_weight_words), (up_words, up_weight_words)):
-                given_bytes = given[g].rearrange("p n t -> p (n t)")
-                nc.sync.dma_start(
-                    out=words[:, g, K_PASS * c : K_PASS * (c + 1)].bitcast(I32),
-                    in_=given_bytes[:, PACK * K_PASS * c : PACK * K_PASS * (c + 1)].bitcast(I32),
-                )
-
-        def load_down(r):
-            g, c = divmod(r, CHUNKS)
-            if c == 0:
-                load_planes(down_scales[:, g, :], down_weight_scales[CHUNKS * g : CHUNKS * (g + 1)])
+        def load_planes(weight, g, quadrant):
+            words, planes, given_bytes, given_rows = weight
             nc.sync.dma_start(
-                out=down_words[:, r, :].bitcast(I32),
-                in_=down_weight_words[r].rearrange("p n t -> p (n t)").bitcast(I32),
+                out=planes[32 * quadrant : 32 * quadrant + 16, g, :].bitcast(I32),
+                in_=given_rows[g, :, 4 * quadrant : 4 * quadrant + 4, :].bitcast(I32),
             )
 
+        def load_piece(weight, r):
+            g, c = divmod(r, CHUNKS)
+            words, planes, given_bytes, given_rows = weight
+            nc.sync.dma_start(out=words[:, g, c, :].bitcast(I32), in_=given_bytes[g, c].bitcast(I32))
+            if g + 1 < GROUPS:
+                load_planes(weight, g + 1, c)
+
         nc.sync.dma_start(out=x_rows[:, 0], in_=x_view[0])
-        for r in range(ROUNDS + 1):
+        for quadrant in range(QUADRANTS):
+            load_planes(gate, 0, quadrant)
+        load_piece(gate, 0)
+        load_piece(up, 0)
+        for quadrant in range(QUADRANTS):
+            load_planes(up, 0, quadrant)
+        for r in range(1, ROUNDS + 1):
             if r < ROUNDS:
-                load_gate_up(r)
-            if 1 <= r < GROUPS:
+                load_piece(gate, r)
+                load_piece(up, r)
+            if r < GROUPS:
                 nc.sync.dma_start(out=x_rows[:, r], in_=x_view[r])
-            if r >= 1:
-                load_down(r - 1)
+            if r == 1:
+                for quadrant in range(QUADRANTS):
+                    load_planes(down, 0, quadrant)
+            load_piece(down, r - 1)
 
         gate_up_banks = ctx.enter_context(tc.psum_pool(name="gate_up_banks", bufs=ROW_TILES))
         turned_banks = ctx.enter_context(tc.psum_pool(name="turned_banks", bufs=2))
@@ -119,7 +128,6 @@ def tile_groupedmlp_plana_e_kernel(
 
         def gate_up_passes(r):
             g, c = divmod(r, CHUNKS)
-            cols = slice(K_PASS * c, K_PASS * (c + 1))
             for sums, words, planes, name in (
                 (gate_sums, gate_words, gate_scales, "gate_bank"),
                 (up_sums, up_words, up_scales, "up_bank"),
@@ -131,7 +139,7 @@ def tile_groupedmlp_plana_e_kernel(
                         out=sums[bt][:],
                         lhsT=x_words[:, g, rows].bitcast(FP8X4),
                         lhsT_scale=x_scales[:, g, rows],
-                        rhs=words[:, g, cols].bitcast(FP8X4),
+                        rhs=words[:, g, c, :].bitcast(FP8X4),
                         rhs_scale=planes[4 * c : P, g, :],
                         start=True,
                         stop=True,
@@ -196,7 +204,7 @@ def tile_groupedmlp_plana_e_kernel(
                     out=down_sums[bt][:],
                     lhsT=codes[:, rows].bitcast(FP8X4),
                     lhsT_scale=scales[:, rows],
-                    rhs=down_words[:, r, :].bitcast(FP8X4),
+                    rhs=down_words[:, g, c, :].bitcast(FP8X4),
                     rhs_scale=down_scales[4 * c : P, g, :],
                     start=(c == 0),
                     stop=(c == CHUNKS - 1),

@@ -27,6 +27,7 @@ ROW_TILES = ROWS // P
 CHUNKS = D_HID // K_PASS
 ROUNDS = GROUPS * CHUNKS
 DOWN_LAG = 3
+X_LEAD = 2
 
 FLOPS = 2 * GROUPS * ROWS * (2 * D_IN * D_HID + D_HID * D_OUT)
 
@@ -110,16 +111,17 @@ def tile_groupedmlp_plana_e_kernel(
         load_piece(up, 0)
         for quadrant in range(QUADRANTS):
             load_planes(up, 0, quadrant)
-        for r in range(1, ROUNDS + 1):
+        for r in range(1, ROUNDS + 2):
             if r < ROUNDS:
                 load_piece(gate, r)
                 load_piece(up, r)
-            if r < GROUPS:
-                nc.sync.dma_start(out=x_rows[:, r], in_=x_view[r])
-            if r == 1:
+            if (r + X_LEAD) % CHUNKS == 0 and r + X_LEAD < ROUNDS:
+                nc.sync.dma_start(out=x_rows[:, (r + X_LEAD) // CHUNKS], in_=x_view[(r + X_LEAD) // CHUNKS])
+            if r == 2:
                 for quadrant in range(QUADRANTS):
                     load_planes(down, 0, quadrant)
-            load_piece(down, r - 1)
+            if r >= 2:
+                load_piece(down, r - 2)
 
         gate_up_banks = ctx.enter_context(tc.psum_pool(name="gate_up_banks", bufs=ROW_TILES))
         turned_banks = ctx.enter_context(tc.psum_pool(name="turned_banks", bufs=2))
@@ -161,36 +163,44 @@ def tile_groupedmlp_plana_e_kernel(
                     op=MULT,
                 )
 
-        def turn_and_quantise(word_columns, codes, scales):
-            turned = turned_banks.tile([P, ROW_TILES, PAIRS, P], F32)
-            for bt in range(ROW_TILES):
+        def turn_and_quantise(word_columns, codes, scales, tiles):
+            turned = turned_banks.tile([P, len(tiles), PAIRS, P], F32)
+            for i, bt in enumerate(tiles):
                 for u in range(PAIRS):
-                    nc.tensor.transpose(turned[:, bt, u, :], word_columns(bt, u), identity[:])
-            grouped = work.tile([P, ROW_TILES, P, PACK], BF16, align_bytes=64)
+                    nc.tensor.transpose(turned[:, i, u, :], word_columns(bt, u), identity[:])
+            grouped = work.tile([P, len(tiles), P, PACK], BF16, align_bytes=64)
             nc.scalar.copy(
                 out=grouped[:].bitcast(F32), in_=turned[:].rearrange("p bt u b -> p bt b u")
             )
+            rows = slice(P * tiles.start, P * tiles.stop)
             nc.vector.quantize_mx(
-                out=codes.bitcast(FP8X4),
-                scales=scales,
+                out=codes[:, rows].bitcast(FP8X4),
+                scales=scales[:, rows],
                 in_=grouped[:].rearrange("p bt b t -> p (bt b t)"),
             )
 
-        def turn_and_quantise_x(g):
+        def turn_and_quantise_x(g, tiles):
             turn_and_quantise(
                 lambda bt, u: x_rows[:, g, bt, :].bitcast(F32)[:, u : D_IN // 2 : PAIRS],
                 x_words[:, g, :],
                 x_scales[:, g, :],
+                tiles,
             )
 
         def turn_and_quantise_hidden(r):
             codes = work.tile([P, ROWS], U32, align_bytes=64, bufs=DOWN_LAG)
             scales = work.tile([P, ROWS], U8, align_bytes=64, bufs=DOWN_LAG)
-            turn_and_quantise(
-                lambda bt, u: hidden[r, bt][:, u].rearrange("b p e -> b (p e)").bitcast(F32),
-                codes[:],
-                scales[:],
-            )
+            if r == ROUNDS - 1:
+                parts = [range(bt, bt + 1) for bt in range(ROW_TILES)]
+            else:
+                parts = [range(ROW_TILES)]
+            for tiles in parts:
+                turn_and_quantise(
+                    lambda bt, u: hidden[r, bt][:, u].rearrange("b p e -> b (p e)").bitcast(F32),
+                    codes[:],
+                    scales[:],
+                    tiles,
+                )
             hidden_mx[r] = (codes, scales)
 
         def down_passes(r):
@@ -216,7 +226,8 @@ def tile_groupedmlp_plana_e_kernel(
             for bt in range(ROW_TILES):
                 nc.sync.dma_start(out=out_view[:, bt, g, :], in_=out_rows[:, bt, g, :])
 
-        turn_and_quantise_x(0)
+        for bt in range(ROW_TILES):
+            turn_and_quantise_x(0, range(bt, bt + 1))
         for step in range(ROUNDS + DOWN_LAG):
             if step < ROUNDS:
                 gate_up_passes(step)
@@ -228,5 +239,5 @@ def tile_groupedmlp_plana_e_kernel(
                 store_group((step - DOWN_LAG) // CHUNKS)
             if 1 <= step <= ROUNDS:
                 turn_and_quantise_hidden(step - 1)
-            if 1 <= step < GROUPS:
-                turn_and_quantise_x(step)
+            if (step + X_LEAD) % CHUNKS == 0 and step + X_LEAD < ROUNDS:
+                turn_and_quantise_x((step + X_LEAD) // CHUNKS, range(ROW_TILES))

@@ -229,14 +229,13 @@ def tile_groupedmlp_plana_e_kernel(
         for bt in range(ROW_TILES):
             turn_and_quantise_x(0, range(bt, bt + 1))
         for step in range(ROUNDS + DOWN_LAG):
-            if step < ROUNDS:
-                gate_up_passes(step)
             if step >= DOWN_LAG:
                 down_passes(step - DOWN_LAG)
+                if (step - DOWN_LAG) % CHUNKS == CHUNKS - 1:
+                    store_group((step - DOWN_LAG) // CHUNKS)
             if step < ROUNDS:
+                gate_up_passes(step)
                 swiglu(step)
-            if step >= DOWN_LAG and (step - DOWN_LAG) % CHUNKS == CHUNKS - 1:
-                store_group((step - DOWN_LAG) // CHUNKS)
             if 1 <= step <= ROUNDS:
                 turn_and_quantise_hidden(step - 1)
             if (step + X_LEAD) % CHUNKS == 0 and step + X_LEAD < ROUNDS:

@@ -65,9 +65,12 @@ def tile_groupedmlp_plana_e_kernel(
         x_view = x.rearrange("(bt p g) d -> g p bt d", bt=ROW_TILES, p=P, g=GROUPS)
         out_view = out.rearrange("(bt p g) o -> p bt g o", bt=ROW_TILES, p=P, g=GROUPS)
 
-        for planes in (gate_scales, up_scales, down_scales):
-            nc.vector.memset(planes[:].bitcast(I32), 0)
+        for planes in (gate_scales, up_scales):
+            nc.gpsimd.memset(planes[:, 0, :].bitcast(F32), 0.0)
         make_identity(nc, identity[:])
+        for planes in (gate_scales, up_scales):
+            nc.vector.memset(planes[:, 1:GROUPS, :].rearrange("p g n -> p (g n)").bitcast(I32), 0)
+        nc.vector.memset(down_scales[:].bitcast(I32), 0)
         nc.vector.memset(warm[:], 0.0)
         nc.scalar.activation(out=warm[:, 1:2], in_=warm[:, 0:1], func=SILU)
 

from contextlib import ExitStack

import concourse.mybir as mybir
from concourse.masks import make_identity

F32 = mybir.dt.float32
BF16 = mybir.dt.bfloat16
I32 = mybir.dt.int32
U32 = mybir.dt.uint32
U8 = mybir.dt.uint8
FP8X4 = mybir.dt.float8_e4m3fn_x4
SILU = mybir.ActivationFunctionType.Silu
MULT = mybir.AluOpType.mult

P = 128
PACK = 4
PAIRS = 2
K_PASS = P * PACK
QUADRANTS = 4

GROUPS = 4
ROWS = 256
D_IN = 512
D_HID = 2048
D_OUT = 512
ROW_TILES = ROWS // P
CHUNKS = D_HID // K_PASS
ROUNDS = GROUPS * CHUNKS
DOWN_LAG = 3
X_LEAD = 2

FLOPS = 2 * GROUPS * ROWS * (2 * D_IN * D_HID + D_HID * D_OUT)


def tile_groupedmlp_plana_e_kernel(
    tc,
    x,
    gate_weight_words,
    gate_weight_scales,
    up_weight_words,
    up_weight_scales,
    down_weight_words,
    down_weight_scales,
    out,
):
    nc = tc.nc
    with ExitStack() as ctx:
        ctx.enter_context(tc.manual_schedule())
        keep = ctx.enter_context(tc.tile_pool(name="keep", bufs=1))
        work = ctx.enter_context(tc.tile_pool(name="work", bufs=2))

        x_rows = keep.tile([P, GROUPS, ROW_TILES, D_IN], BF16)
        x_words = keep.tile([P, GROUPS, ROWS], U32, align_bytes=64)
        x_scales = keep.tile([P, GROUPS, ROWS], U8, align_bytes=64)
        gate_words = keep.tile([P, GROUPS, CHUNKS, K_PASS], U32, align_bytes=64)
        up_words = keep.tile([P, GROUPS, CHUNKS, K_PASS], U32, align_bytes=64)
        down_words = keep.tile([P, GROUPS, CHUNKS, D_OUT], U32, align_bytes=64)
        gate_scales = keep.tile([P, GROUPS, K_PASS], U8, align_bytes=64)
        up_scales = keep.tile([P, GROUPS, K_PASS], U8, align_bytes=64)
        down_scales = keep.tile([P, GROUPS, D_OUT], U8, align_bytes=64)
        out_rows = keep.tile([P, ROW_TILES, GROUPS, D_OUT], F32)
        identity = keep.tile([P, P], F32)
        warm = keep.tile([P, 2], F32)

        x_view = x.rearrange("(bt p g) d -> g p bt d", bt=ROW_TILES, p=P, g=GROUPS)
        out_view = out.rearrange("(bt p g) o -> p bt g o", bt=ROW_TILES, p=P, g=GROUPS)

        for planes in (gate_scales, up_scales):
            nc.gpsimd.memset(planes[:, 0, :].bitcast(F32), 0.0)
        make_identity(nc, identity[:])
        for planes in (gate_scales, up_scales):
            nc.vector.memset(planes[:, 1:GROUPS, :].rearrange("p g n -> p (g n)").bitcast(I32), 0)
        nc.vector.memset(down_scales[:].bitcast(I32), 0)
        nc.vector.memset(warm[:], 0.0)
        nc.scalar.activation(out=warm[:, 1:2], in_=warm[:, 0:1], func=SILU)

        gate = (
            gate_words,
            gate_scales,
            gate_weight_words.rearrange("g p (c n) t -> g c p (n t)", c=CHUNKS),
            gate_weight_scales.rearrange("g q (c n) -> g c q n", c=CHUNKS),
        )
        up = (
            up_words,
            up_scales,
            up_weight_words.rearrange("g p (c n) t -> g c p (n t)", c=CHUNKS),
            up_weight_scales.rearrange("g q (c n) -> g c q n", c=CHUNKS),
        )
        down = (
            down_words,
            down_scales,
            down_weight_words.rearrange("(g c) p n t -> g c p (n t)", c=CHUNKS),
            down_weight_scales.rearrange("(g c) q n -> g c q n", c=CHUNKS),
        )

        def load_planes(weight, g, quadrant):
            words, planes, given_bytes, given_rows = weight
            nc.sync.dma_start(
                out=planes[32 * quadrant : 32 * quadrant + 16, g, :].bitcast(I32),
                in_=given_rows[g, :, 4 * quadrant : 4 * quadrant + 4, :].bitcast(I32),
            )

        def load_piece(weight, r):
            g, c = divmod(r, CHUNKS)
            words, planes, given_bytes, given_rows = weight
            nc.sync.dma_start(out=words[:, g, c, :].bitcast(I32), in_=given_bytes[g, c].bitcast(I32))
            if g + 1 < GROUPS:
                load_planes(weight, g + 1, c)

        nc.sync.dma_start(out=x_rows[:, 0], in_=x_view[0])
        for quadrant in range(QUADRANTS):
            load_planes(gate, 0, quadrant)
        load_piece(gate, 0)
        load_piece(up, 0)
        for quadrant in range(QUADRANTS):
            load_planes(up, 0, quadrant)
        for r in range(1, ROUNDS + 2):
            if r < ROUNDS:
                load_piece(gate, r)
                load_piece(up, r)
            if (r + X_LEAD) % CHUNKS == 0 and r + X_LEAD < ROUNDS:
                nc.sync.dma_start(out=x_rows[:, (r + X_LEAD) // CHUNKS], in_=x_view[(r + X_LEAD) // CHUNKS])
            if r == 2:
                for quadrant in range(QUADRANTS):
                    load_planes(down, 0, quadrant)
            if r >= 2:
                load_piece(down, r - 2)

        gate_up_banks = ctx.enter_context(tc.psum_pool(name="gate_up_banks", bufs=ROW_TILES))
        turned_banks = ctx.enter_context(tc.psum_pool(name="turned_banks", bufs=2))
        down_banks = ctx.enter_context(tc.psum_pool(name="down_banks", bufs=ROW_TILES))
        gate_sums, up_sums, hidden, hidden_mx, down_sums = {}, {}, {}, {}, {}

        def gate_up_passes(r):
            g, c = divmod(r, CHUNKS)
            for sums, words, planes, name in (
                (gate_sums, gate_words, gate_scales, "gate_bank"),
                (up_sums, up_words, up_scales, "up_bank"),
            ):
                for bt in range(ROW_TILES):
                    rows = slice(P * bt, P * (bt + 1))
                    sums[bt] = gate_up_banks.tile([P, K_PASS], F32, name=name)
                    nc.tensor.matmul_mx(
                        out=sums[bt][:],
                        lhsT=x_words[:, g, rows].bitcast(FP8X4),
                        lhsT_scale=x_scales[:, g, rows],
                        rhs=words[:, g, c, :].bitcast(FP8X4),
                        rhs_scale=planes[4 * c : P, g, :],
                        start=True,
                        stop=True,
                    )

        def swiglu(r):
            for bt in range(ROW_TILES):
                silu_gate = work.tile([P, PAIRS, P, 2], F32)
                nc.scalar.activation(
                    out=silu_gate[:],
                    in_=gate_sums[bt][:].rearrange("b (p u e) -> b u p e", u=PAIRS, e=2),
                    func=SILU,
                )
                hidden[r, bt] = work.tile([P, PAIRS, P, 2], BF16, name="hidden", bufs=2 * ROW_TILES)
                nc.vector.tensor_tensor(
                    out=hidden[r, bt][:],
                    in0=up_sums[bt][:].rearrange("b (p u e) -> b u p e", u=PAIRS, e=2),
                    in1=silu_gate[:],
                    op=MULT,
                )

        def turn_and_quantise(word_columns, codes, scales, tiles):
            turned = turned_banks.tile([P, len(tiles), PAIRS, P], F32)
            for i, bt in enumerate(tiles):
                for u in range(PAIRS):
                    nc.tensor.transpose(turned[:, i, u, :], word_columns(bt, u), identity[:])
            grouped = work.tile([P, len(tiles), P, PACK], BF16, align_bytes=64)
            nc.scalar.copy(
                out=grouped[:].bitcast(F32), in_=turned[:].rearrange("p bt u b -> p bt b u")
            )
            rows = slice(P * tiles.start, P * tiles.stop)
            nc.vector.quantize_mx(
                out=codes[:, rows].bitcast(FP8X4),
                scales=scales[:, rows],
                in_=grouped[:].rearrange("p bt b t -> p (bt b t)"),
            )

        def turn_and_quantise_x(g, tiles):
            turn_and_quantise(
                lambda bt, u: x_rows[:, g, bt, :].bitcast(F32)[:, u : D_IN // 2 : PAIRS],
                x_words[:, g, :],
                x_scales[:, g, :],
                tiles,
            )

        def turn_and_quantise_hidden(r):
            codes = work.tile([P, ROWS], U32, align_bytes=64, bufs=DOWN_LAG)
            scales = work.tile([P, ROWS], U8, align_bytes=64, bufs=DOWN_LAG)
            if r == ROUNDS - 1:
                parts = [range(bt, bt + 1) for bt in range(ROW_TILES)]
            else:
                parts = [range(ROW_TILES)]
            for tiles in parts:
                turn_and_quantise(
                    lambda bt, u: hidden[r, bt][:, u].rearrange("b p e -> b (p e)").bitcast(F32),
                    codes[:],
                    scales[:],
                    tiles,
                )
            hidden_mx[r] = (codes, scales)

        def down_passes(r):
            g, c = divmod(r, CHUNKS)
            codes, scales = hidden_mx[r]
            for bt in range(ROW_TILES):
                rows = slice(P * bt, P * (bt + 1))
                if c == 0:
                    down_sums[bt] = down_banks.tile([P, D_OUT], F32, name="down_bank")
                nc.tensor.matmul_mx(
                    out=down_sums[bt][:],
                    lhsT=codes[:, rows].bitcast(FP8X4),
                    lhsT_scale=scales[:, rows],
                    rhs=down_words[:, g, c, :].bitcast(FP8X4),
                    rhs_scale=down_scales[4 * c : P, g, :],
                    start=(c == 0),
                    stop=(c == CHUNKS - 1),
                )

        def store_group(g):
            nc.scalar.copy(out=out_rows[:, 0, g, :], in_=down_sums[0][:])
            nc.vector.tensor_copy(out=out_rows[:, 1, g, :], in_=down_sums[1][:])
            for bt in range(ROW_TILES):
                nc.sync.dma_start(out=out_view[:, bt, g, :], in_=out_rows[:, bt, g, :])

        for bt in range(ROW_TILES):
            turn_and_quantise_x(0, range(bt, bt + 1))
        for step in range(ROUNDS + DOWN_LAG):
            if step >= DOWN_LAG:
                down_passes(step - DOWN_LAG)
                if (step - DOWN_LAG) % CHUNKS == CHUNKS - 1:
                    store_group((step - DOWN_LAG) // CHUNKS)
            if step < ROUNDS:
                gate_up_passes(step)
                swiglu(step)
            if 1 <= step <= ROUNDS:
                turn_and_quantise_hidden(step - 1)
            if (step + X_LEAD) % CHUNKS == 0 and step + X_LEAD < ROUNDS:
                turn_and_quantise_x((step + X_LEAD) // CHUNKS, range(ROW_TILES))
